import numpy as np
import ml_dtypes


def mxq(x, axis, fmt="e4m3"):
    dtype, down = {"e4m3": (ml_dtypes.float8_e4m3fn, 7), "e5m2": (ml_dtypes.float8_e5m2, 14)}[fmt]
    v = np.moveaxis(np.asarray(x, np.float32).astype(ml_dtypes.bfloat16).astype(np.float64), axis, -1)
    blocks = v.reshape(v.shape[:-1] + (-1, 32))
    amax = np.abs(blocks).max(-1, keepdims=True)
    byte = np.maximum(np.where(amax > 0, np.frexp(amax)[1] - 1 + 127, 0) - down, 1)
    scale = np.exp2(byte - 127.0)
    codes = (blocks / scale).astype(np.float32).astype(dtype).astype(np.float64)
    return np.moveaxis((codes * scale).reshape(v.shape), -1, axis)


WIDE = False


def mx_kscale(k):
    if not WIDE:
        return np.ones(k)
    levels = np.array([10, -10, 5, -5, 0])
    a = np.random.permutation(np.resize(levels, k // 512 * 4)).reshape(k // 512, 4)
    idx = np.arange(k)
    return np.exp2(a[idx // 512, idx % 128 // 32])


BF16 = ml_dtypes.bfloat16


def bf(x):
    return np.asarray(x, np.float32).astype(BF16)


def f64(x):
    return np.asarray(x).astype(np.float64)


C, S, L, D, NK = 32, 256, 3, 128, 12
COUNTS = [len(range(h, NK, L)) for h in range(L)]


def setup_inputs():
    s = mx_kscale(C * D).reshape(C, D)
    inp = {'Ec': bf(np.random.standard_normal((C, S, L, D)) * s[:, None, None, :])}
    for h in range(1, L + 1):
        inp['W%d' % h] = bf(np.random.standard_normal((COUNTS[h - 1], C, C, h, D)) / np.sqrt(C * h * D) / s[None, None, :, None, :])
    for h in range(1, L + 1):
        inp['b%d' % h] = bf(np.random.standard_normal((COUNTS[h - 1], C)) * 0.3)
    return inp


def reference(Ec, W1, W2, W3, b1, b2, b3):
    Ec_t = np.transpose(f64(Ec), (1, 0, 2, 3))
    Ws = [f64(W1), f64(W2), f64(W3)]
    bs = [f64(b1), f64(b2), f64(b3)]
    res = [None] * NK
    for h_idx in range(L):
        h = h_idx + 1
        P = L - h + 1
        idxs = list(range(h_idx, NK, L))
        k = len(idxs)
        windows = np.stack([Ec_t[:, :, p:p + h, :] for p in range(P)], axis=0)
        a = mxq(windows.reshape(P * S, C * h * D), 1, 'e4m3')
        w = mxq(Ws[h_idx].reshape(k * C, C * h * D), 1, 'e4m3')
        conv = (a @ w.T).reshape(P, S, k, C).transpose(0, 2, 1, 3)
        conv = conv + bs[h_idx][None, :, None, :]
        pooled = np.maximum(np.max(conv, axis=0), 0.0)
        for j, idx in enumerate(idxs):
            res[idx] = pooled[j]
    out = np.stack(res, axis=-1)
    return np.transpose(out, (1, 0, 2))[:, :, None, :]

@@ -1,0 +1,165 @@
+from contextlib import ExitStack
+
+import concourse.mybir as mybir
+from concourse.masks import make_identity
+
+BF16 = mybir.dt.bfloat16
+F32 = mybir.dt.float32
+U32 = mybir.dt.uint32
+U8 = mybir.dt.uint8
+FP8X4 = mybir.dt.float8_e4m3fn_x4
+ALU = mybir.AluOpType
+ACT = mybir.ActivationFunctionType
+AX = mybir.AxisListType
+
+P = 128
+C, S, L, D = 32, 256, 3, 128
+CS = 4
+G = C // CS
+FLOPS = 2 * 128 * (768 * 4096 + 512 * 8192 + 256 * 12288)
+
+
+def tile_vrtconv_kernel(tc, Ec, W1, W2, W3, b1, b2, b3, out):
+    nc = tc.nc
+    with ExitStack() as ctx:
+        const = ctx.enter_context(tc.tile_pool(name="const", bufs=1))
+        ld = ctx.enter_context(tc.tile_pool(name="ld", bufs=G))
+        rg = ctx.enter_context(tc.tile_pool(name="rg", bufs=2))
+        grp = ctx.enter_context(tc.tile_pool(name="grp", bufs=2))
+        keep = ctx.enter_context(tc.tile_pool(name="keep", bufs=3))
+        accp = ctx.enter_context(tc.psum_pool(name="accp", bufs=1))
+        tpp = ctx.enter_context(tc.psum_pool(name="tpp", bufs=4))
+
+        ec_v = Ec.rearrange("c (p q) l d -> p c (q l d)", q=2)
+        w_v = [w.rearrange("j o c a d -> (j o) (c a d)") for w in (W1, W2, W3)]
+
+        bz = const.tile([P, P], BF16, name="bz")
+        nc.vector.memset(bz[:], 0.0)
+        for h, b in enumerate((b1, b2, b3)):
+            nc.scalar.dma_start(out=bz[h:h + 1, :], in_=b.rearrange("(x j) o -> x (j o)", x=1))
+
+        nat = []
+        for g in range(G):
+            en = ld.tile([P, CS, 6 * D], BF16, name="en", tag="en")
+            nc.sync.dma_start(out=en[:], in_=ec_v[:, g * CS:(g + 1) * CS, :])
+            wn = []
+            for h in range(3):
+                wid = CS * (h + 1) * D
+                t = ld.tile([P, wid], BF16, name="wn%d" % h, tag="wn%d" % h)
+                nc.sync.dma_start(out=t[:], in_=w_v[h][:, g * wid:(g + 1) * wid])
+                wn.append(t)
+            nat.append((en, wn))
+
+        identf = const.tile([P, P], F32, name="identf")
+        make_identity(nc, identf[:])
+        identb = const.tile([P, P], BF16, name="identb")
+        make_identity(nc, identb[:])
+        bias = const.tile([P, 4], F32, name="bias")
+
+        acc_a = accp.tile([P, 512], F32, name="acc_a")
+        acc_b = accp.tile([P, 256], F32, name="acc_b")
+        acc_c = accp.tile([P, 512], F32, name="acc_c")
+        acc_d = accp.tile([P, 256], F32, name="acc_d")
+
+        state = {}
+
+        def regroup(g):
+            en, wn = nat[g]
+            er = rg.tile([P, 6, CS, D], BF16, name="er", tag="er")
+            nc.vector.tensor_copy(out=er[:], in_=en[:].rearrange("p c (r d) -> p r c d", d=D))
+            w2r = rg.tile([P, 2, CS, D], BF16, name="w2r", tag="w2r")
+            nc.vector.tensor_copy(out=w2r[:], in_=wn[1][:].rearrange("p (c a d) -> p a c d", a=2, d=D))
+            w3r = rg.tile([P, 3, CS, D], BF16, name="w3r", tag="w3r")
+            nc.vector.tensor_copy(out=w3r[:], in_=wn[2][:].rearrange("p (c a d) -> p a c d", a=3, d=D))
+            state[("r", g)] = (
+                er[:].rearrange("p r c d -> p (r c d)").bitcast(F32),
+                wn[0][:].bitcast(F32),
+                w2r[:].rearrange("p a c d -> p (a c d)").bitcast(F32),
+                w3r[:].rearrange("p a c d -> p (a c d)").bitcast(F32),
+            )
+
+        def transposes(g):
+            erf, w1f, w2f, w3f = state[("r", g)]
+            gr = grp.tile([P, 6 * 1024], BF16, name="gr", tag="gr", align_bytes=64)
+            grf = gr[:].bitcast(F32).rearrange("p (n x c u) -> p n x c u", n=6, x=2, u=2)
+            stat = [(w1f, 0), (w2f, 0), (w2f, 1), (w3f, 0), (w3f, 1), (w3f, 2)]
+            for n in range(6):
+                tp = tpp.tile([P, 2, 2, P], F32, name="tp", tag="tp")
+                for x in range(2):
+                    for u in range(2):
+                        if n < 3:
+                            src, win = erf, (3 * x + n) * 2 + u
+                        else:
+                            src, a = stat[2 * (n - 3) + x]
+                            win = a * 2 + u
+                        nc.tensor.transpose(out=tp[:, x, u, :], in_=src[:, win * P:(win + 1) * P], identity=identf[:])
+                nc.scalar.copy(out=grf[:, n], in_=tp[:].rearrange("p x u c -> p x c u"))
+            state[("g", g)] = gr
+
+        def quantise(g):
+            gr = state[("g", g)]
+            cd = keep.tile([P, 1536], U32, name="cd", tag="cd", align_bytes=64)
+            sc = keep.tile([P, 1536], U8, name="sc", tag="sc", align_bytes=64)
+            nc.vector.quantize_mx(out=cd[:, 0:1024].bitcast(FP8X4), scales=sc[:, 0:1024], in_=gr[:, 0:4096])
+            nc.vector.quantize_mx(out=cd[:, 1024:1536].bitcast(FP8X4), scales=sc[:, 1024:1536], in_=gr[:, 4096:6144])
+            state[("q", g)] = (cd, sc)
+
+        def passes(g):
+            cd, sc = state[("q", g)]
+            first, last = g == 0, g == G - 1
+
+            def mx(acc, i, lo, hi, start, stop):
+                w0 = 768 + P * i
+                nc.tensor.matmul_mx(
+                    out=acc[:],
+                    lhsT=cd[:, w0:w0 + P].bitcast(FP8X4), lhsT_scale=sc[:, w0:w0 + P],
+                    rhs=cd[:, lo:hi].bitcast(FP8X4), rhs_scale=sc[:, lo:hi],
+                    start=start, stop=stop,
+                )
+
+            mx(acc_a, 0, 0, 512, first, last)
+            mx(acc_b, 0, 512, 768, first, last)
+            mx(acc_c, 1, 0, 512, first, False)
+            mx(acc_c, 2, 256, 768, False, last)
+            mx(acc_d, 3, 0, 256, first, False)
+            mx(acc_d, 4, 256, 512, False, False)
+            mx(acc_d, 5, 512, 768, False, last)
+
+        regroup(0)
+        transposes(0)
+        for g in range(G):
+            if g + 1 < G:
+                regroup(g + 1)
+                transposes(g + 1)
+            quantise(g)
+            passes(g)
+            if g == 3:
+                tpb = tpp.tile([P, P], BF16, name="tpb", tag="tp")
+                nc.tensor.transpose(out=tpb[:], in_=bz[:], identity=identb[:])
+                nc.vector.tensor_copy(out=bias[:, 0:3], in_=tpb[:, 0:3])
+
+        res = []
+        t1 = const.tile([P, 256], F32, name="t1")
+        nc.vector.tensor_reduce(out=t1[:], in_=acc_a[:].rearrange("p (t n) -> p n t", t=2), axis=AX.X, op=ALU.max)
+        t1b = const.tile([P, 256], F32, name="t1b")
+        nc.vector.tensor_tensor(out=t1b[:], in0=t1[:], in1=acc_b[:], op=ALU.max)
+        t2 = const.tile([P, 256], F32, name="t2")
+        nc.vector.tensor_reduce(out=t2[:], in_=acc_c[:].rearrange("p (t n) -> p n t", t=2), axis=AX.X, op=ALU.max)
+        for h, src in enumerate((t1b, t2, acc_d)):
+            r = const.tile([P, 256], F32, name="r%d" % h)
+            nc.scalar.activation(out=r[:], in_=src[:], func=ACT.Relu, bias=bias[:, h:h + 1], scale=1.0)
+            res.append(r)
+
+        gout = const.tile([P, 32, 2, 12], F32, name="gout")
+        for q in range(2):
+            tf = tpp.tile([P, 3, P], F32, name="tf", tag="tp")
+            for h in range(3):
+                nc.tensor.transpose(out=tf[:, h, :], in_=res[h][:, q * P:(q + 1) * P], identity=identf[:])
+            nc.vector.tensor_copy(
+                out=gout[:, :, q, :].rearrange("p o (j h) -> p o j h", h=3),
+                in_=tf[:].rearrange("p h (j o) -> p o j h", o=32),
+            )
+        nc.sync.dma_start(
+            out=out.rearrange("o (p q) z k -> p o (q z k)", q=2),
+            in_=gout[:].rearrange("p o q k -> p o (q k)"),
+        )

@@ -63,27 +63,34 @@ def tile_vrtconv_kernel(tc, Ec, W1, W2, W3, b1, b2, b3, out):
 
         state = {}
 
-        def regroup(g):
-            en, wn = nat[g]
+        def regroup_e(g):
+            en = nat[g][0]
             er = rg.tile([P, 6, CS, D], BF16, name="er", tag="er")
             nc.vector.tensor_copy(out=er[:], in_=en[:].rearrange("p c (r d) -> p r c d", d=D))
+            state[("re", g)] = er[:].rearrange("p r c d -> p (r c d)").bitcast(F32)
+
+        def regroup_w(g):
+            wn = nat[g][1]
             w2r = rg.tile([P, 2, CS, D], BF16, name="w2r", tag="w2r")
             nc.vector.tensor_copy(out=w2r[:], in_=wn[1][:].rearrange("p (c a d) -> p a c d", a=2, d=D))
             w3r = rg.tile([P, 3, CS, D], BF16, name="w3r", tag="w3r")
             nc.vector.tensor_copy(out=w3r[:], in_=wn[2][:].rearrange("p (c a d) -> p a c d", a=3, d=D))
-            state[("r", g)] = (
-                er[:].rearrange("p r c d -> p (r c d)").bitcast(F32),
+            state[("rw", g)] = (
                 wn[0][:].bitcast(F32),
                 w2r[:].rearrange("p a c d -> p (a c d)").bitcast(F32),
                 w3r[:].rearrange("p a c d -> p (a c d)").bitcast(F32),
             )
 
-        def transposes(g):
-            erf, w1f, w2f, w3f = state[("r", g)]
-            gr = grp.tile([P, 6 * 1024], BF16, name="gr", tag="gr", align_bytes=64)
+        def transposes(g, lo, hi):
+            if lo == 0:
+                gr = grp.tile([P, 6 * 1024], BF16, name="gr", tag="gr", align_bytes=64)
+                state[("g", g)] = gr
+            gr = state[("g", g)]
+            erf = state[("re", g)]
+            w1f, w2f, w3f = state.get(("rw", g), (None, None, None))
             grf = gr[:].bitcast(F32).rearrange("p (n x c u) -> p n x c u", n=6, x=2, u=2)
             stat = [(w1f, 0), (w2f, 0), (w2f, 1), (w3f, 0), (w3f, 1), (w3f, 2)]
-            for n in range(6):
+            for n in range(lo, hi):
                 tp = tpp.tile([P, 2, 2, P], F32, name="tp", tag="tp")
                 for x in range(2):
                     for u in range(2):
@@ -94,17 +101,19 @@ def tile_vrtconv_kernel(tc, Ec, W1, W2, W3, b1, b2, b3, out):
                             win = a * 2 + u
                         nc.tensor.transpose(out=tp[:, x, u, :], in_=src[:, win * P:(win + 1) * P], identity=identf[:])
                 nc.scalar.copy(out=grf[:, n], in_=tp[:].rearrange("p x u c -> p x c u"))
-            state[("g", g)] = gr
 
-        def quantise(g):
+        def quantise(g, half):
             gr = state[("g", g)]
-            cd = keep.tile([P, 1536], U32, name="cd", tag="cd", align_bytes=64)
-            sc = keep.tile([P, 1536], U8, name="sc", tag="sc", align_bytes=64)
-            nc.vector.quantize_mx(out=cd[:, 0:1024].bitcast(FP8X4), scales=sc[:, 0:1024], in_=gr[:, 0:4096])
-            nc.vector.quantize_mx(out=cd[:, 1024:1536].bitcast(FP8X4), scales=sc[:, 1024:1536], in_=gr[:, 4096:6144])
-            state[("q", g)] = (cd, sc)
+            if half == 0:
+                cd = keep.tile([P, 1536], U32, name="cd", tag="cd", align_bytes=64)
+                sc = keep.tile([P, 1536], U8, name="sc", tag="sc", align_bytes=64)
+                state[("q", g)] = (cd, sc)
+                nc.vector.quantize_mx(out=cd[:, 0:1024].bitcast(FP8X4), scales=sc[:, 0:1024], in_=gr[:, 0:4096])
+            else:
+                cd, sc = state[("q", g)]
+                nc.vector.quantize_mx(out=cd[:, 1024:1536].bitcast(FP8X4), scales=sc[:, 1024:1536], in_=gr[:, 4096:6144])
 
-        def passes(g):
+        def passes(g, half):
             cd, sc = state[("q", g)]
             first, last = g == 0, g == G - 1
 
@@ -117,38 +126,56 @@ def tile_vrtconv_kernel(tc, Ec, W1, W2, W3, b1, b2, b3, out):
                     start=start, stop=stop,
                 )
 
-            mx(acc_a, 0, 0, 512, first, last)
-            mx(acc_b, 0, 512, 768, first, last)
-            mx(acc_c, 1, 0, 512, first, False)
-            mx(acc_c, 2, 256, 768, False, last)
-            mx(acc_d, 3, 0, 256, first, False)
-            mx(acc_d, 4, 256, 512, False, False)
-            mx(acc_d, 5, 512, 768, False, last)
+            if half == 0:
+                mx(acc_a, 0, 0, 512, first, last)
+                mx(acc_b, 0, 512, 768, first, last)
+                mx(acc_c, 1, 0, 512, first, False)
+            else:
+                mx(acc_c, 2, 256, 768, False, last)
+                mx(acc_d, 3, 0, 256, first, False)
+                mx(acc_d, 4, 256, 512, False, False)
+                mx(acc_d, 5, 512, 768, False, last)
 
-        regroup(0)
-        transposes(0)
+        ctx.enter_context(tc.manual_schedule())
+        regroup_e(0)
+        transposes(0, 0, 3)
+        regroup_w(0)
+        transposes(0, 3, 6)
+        regroup_e(1)
+        transposes(1, 0, 3)
         for g in range(G):
+            quantise(g, 0)
+            passes(g, 0)
             if g + 1 < G:
-                regroup(g + 1)
-                transposes(g + 1)
-            quantise(g)
-            passes(g)
+                regroup_w(g + 1)
+                transposes(g + 1, 3, 6)
+            quantise(g, 1)
+            passes(g, 1)
+            if g + 2 < G:
+                regroup_e(g + 2)
+                transposes(g + 2, 0, 3)
             if g == 3:
                 tpb = tpp.tile([P, P], BF16, name="tpb", tag="tp")
                 nc.tensor.transpose(out=tpb[:], in_=bz[:], identity=identb[:])
-                nc.vector.tensor_copy(out=bias[:, 0:3], in_=tpb[:, 0:3])
+                nc.scalar.copy(out=bias[:, 0:3], in_=tpb[:, 0:3])
 
-        res = []
-        t1 = const.tile([P, 256], F32, name="t1")
-        nc.vector.tensor_reduce(out=t1[:], in_=acc_a[:].rearrange("p (t n) -> p n t", t=2), axis=AX.X, op=ALU.max)
-        t1b = const.tile([P, 256], F32, name="t1b")
-        nc.vector.tensor_tensor(out=t1b[:], in0=t1[:], in1=acc_b[:], op=ALU.max)
-        t2 = const.tile([P, 256], F32, name="t2")
-        nc.vector.tensor_reduce(out=t2[:], in_=acc_c[:].rearrange("p (t n) -> p n t", t=2), axis=AX.X, op=ALU.max)
-        for h, src in enumerate((t1b, t2, acc_d)):
-            r = const.tile([P, 256], F32, name="r%d" % h)
-            nc.scalar.activation(out=r[:], in_=src[:], func=ACT.Relu, bias=bias[:, h:h + 1], scale=1.0)
-            res.append(r)
+        def first_pos(name, src, h):
+            t = const.tile([P, 256], F32, name=name)
+            nc.scalar.activation(out=t[:], in_=src, func=ACT.Relu, bias=bias[:, h:h + 1], scale=1.0)
+            return t
+
+        def next_pos(name, src, h, prev):
+            t = const.tile([P, 256], F32, name=name)
+            nc.vector.scalar_tensor_tensor(out=t[:], in0=src, scalar=bias[:, h:h + 1], in1=prev[:], op0=ALU.add, op1=ALU.max)
+            return t
+
+        t1 = first_pos("t1", acc_a[:, 0:256], 0)
+        t1b = next_pos("t1b", acc_a[:, 256:512], 0, t1)
+        r1 = next_pos("r1", acc_b[:], 0, t1b)
+        t2 = first_pos("t2", acc_c[:, 0:256], 1)
+        r2 = next_pos("r2", acc_c[:, 256:512], 1, t2)
+        r3 = first_pos("r3", acc_d[:], 2)
+        res = [r1, r2, r3]
 
         gout = const.tile([P, 32, 2, 12], F32, name="gout")
         for q in range(2):

@@ -7,6 +7,7 @@ BF16 = mybir.dt.bfloat16
 F32 = mybir.dt.float32
 U32 = mybir.dt.uint32
 U8 = mybir.dt.uint8
+I32 = mybir.dt.int32
 FP8X4 = mybir.dt.float8_e4m3fn_x4
 ALU = mybir.AluOpType
 ACT = mybir.ActivationFunctionType
@@ -61,6 +62,22 @@ def tile_vrtconv_kernel(tc, Ec, W1, W2, W3, b1, b2, b3, out):
         acc_c = accp.tile([P, 512], F32, name="acc_c")
         acc_d = accp.tile([P, 256], F32, name="acc_d")
 
+        zb = const.tile([P, 2048], BF16, name="zb", align_bytes=64)
+        nc.vector.memset(zb[:].bitcast(I32), 0)
+        zc = const.tile([P, 640], U32, name="zc", align_bytes=64)
+        zs = const.tile([P, 640], U8, name="zs", align_bytes=64)
+        nc.vector.quantize_mx(out=zc[:, 0:512].bitcast(FP8X4), scales=zs[:, 0:512], in_=zb[:])
+        nc.vector.quantize_mx(out=zc[:, 512:640].bitcast(FP8X4), scales=zs[:, 512:640], in_=zb[:, 0:512])
+
+        def idle_passes(n):
+            for i in range(n):
+                nc.tensor.matmul_mx(
+                    out=acc_a[:],
+                    lhsT=zc[:, 512:640].bitcast(FP8X4), lhsT_scale=zs[:, 512:640],
+                    rhs=zc[:, 0:512].bitcast(FP8X4), rhs_scale=zs[:, 0:512],
+                    start=True, stop=True,
+                )
+
         state = {}
 
         def regroup_e(g):
@@ -108,10 +125,13 @@ def tile_vrtconv_kernel(tc, Ec, W1, W2, W3, b1, b2, b3, out):
                 cd = keep.tile([P, 1536], U32, name="cd", tag="cd", align_bytes=64)
                 sc = keep.tile([P, 1536], U8, name="sc", tag="sc", align_bytes=64)
                 state[("q", g)] = (cd, sc)
-                nc.vector.quantize_mx(out=cd[:, 0:1024].bitcast(FP8X4), scales=sc[:, 0:1024], in_=gr[:, 0:4096])
-            else:
-                cd, sc = state[("q", g)]
-                nc.vector.quantize_mx(out=cd[:, 1024:1536].bitcast(FP8X4), scales=sc[:, 1024:1536], in_=gr[:, 4096:6144])
+            cd, sc = state[("q", g)]
+            lo, hi = (0, 1024) if half == 0 else (1024, 1536)
+            step = (hi - lo) // 2 if g == G - 1 else hi - lo
+            for w in range(lo, hi, step):
+                nc.vector.quantize_mx(
+                    out=cd[:, w:w + step].bitcast(FP8X4), scales=sc[:, w:w + step], in_=gr[:, 4 * w:4 * (w + step)]
+                )
 
         def passes(g, half):
             cd, sc = state[("q", g)]
@@ -137,10 +157,13 @@ def tile_vrtconv_kernel(tc, Ec, W1, W2, W3, b1, b2, b3, out):
                 mx(acc_d, 5, 512, 768, False, last)
 
         ctx.enter_context(tc.manual_schedule())
+        idle_passes(10)
         regroup_e(0)
         transposes(0, 0, 3)
+        idle_passes(2)
         regroup_w(0)
         transposes(0, 3, 6)
+        idle_passes(2)
         regroup_e(1)
         transposes(1, 0, 3)
         for g in range(G):

@@ -11,7 +11,6 @@ I32 = mybir.dt.int32
 FP8X4 = mybir.dt.float8_e4m3fn_x4
 ALU = mybir.AluOpType
 ACT = mybir.ActivationFunctionType
-AX = mybir.AxisListType
 
 P = 128
 C, S, L, D = 32, 256, 3, 128
@@ -34,15 +33,15 @@ def tile_vrtconv_kernel(tc, Ec, W1, W2, W3, b1, b2, b3, out):
         ec_v = Ec.rearrange("c (p q) l d -> p c (q l d)", q=2)
         w_v = [w.rearrange("j o c a d -> (j o) (c a d)") for w in (W1, W2, W3)]
 
-        bz = const.tile([P, P], BF16, name="bz")
-        nc.vector.memset(bz[:], 0.0)
-        for h, b in enumerate((b1, b2, b3)):
-            nc.scalar.dma_start(out=bz[h:h + 1, :], in_=b.rearrange("(x j) o -> x (j o)", x=1))
 
         nat = []
         for g in range(G):
             en = ld.tile([P, CS, 6 * D], BF16, name="en", tag="en")
-            nc.sync.dma_start(out=en[:], in_=ec_v[:, g * CS:(g + 1) * CS, :])
+            if g == 0:
+                for u in range(2):
+                    nc.sync.dma_start(out=en[:, 2 * u:2 * u + 2, :], in_=ec_v[:, 2 * u:2 * u + 2, :])
+            else:
+                nc.sync.dma_start(out=en[:], in_=ec_v[:, g * CS:(g + 1) * CS, :])
             wn = []
             for h in range(3):
                 wid = CS * (h + 1) * D
@@ -56,34 +55,33 @@ def tile_vrtconv_kernel(tc, Ec, W1, W2, W3, b1, b2, b3, out):
         identb = const.tile([P, P], BF16, name="identb")
         make_identity(nc, identb[:])
         bias = const.tile([P, 4], F32, name="bias")
+        bz = const.tile([P, P], BF16, name="bz")
+        nc.gpsimd.memset(bz[:], 0.0)
+        for h, b in enumerate((b1, b2, b3)):
+            nc.gpsimd.dma_start(out=bz[h:h + 1, :], in_=b.rearrange("(x j) o -> x (j o)", x=1))
 
         acc_a = accp.tile([P, 512], F32, name="acc_a")
         acc_b = accp.tile([P, 256], F32, name="acc_b")
         acc_c = accp.tile([P, 512], F32, name="acc_c")
         acc_d = accp.tile([P, 256], F32, name="acc_d")
 
-        zb = const.tile([P, 2048], BF16, name="zb", align_bytes=64)
+        zb = const.tile([P, 512], BF16, name="zb")
         nc.vector.memset(zb[:].bitcast(I32), 0)
-        zc = const.tile([P, 640], U32, name="zc", align_bytes=64)
-        zs = const.tile([P, 640], U8, name="zs", align_bytes=64)
-        nc.vector.quantize_mx(out=zc[:, 0:512].bitcast(FP8X4), scales=zs[:, 0:512], in_=zb[:])
-        nc.vector.quantize_mx(out=zc[:, 512:640].bitcast(FP8X4), scales=zs[:, 512:640], in_=zb[:, 0:512])
 
-        def idle_passes(n):
+        def idle_matmuls(n):
             for i in range(n):
-                nc.tensor.matmul_mx(
-                    out=acc_a[:],
-                    lhsT=zc[:, 512:640].bitcast(FP8X4), lhsT_scale=zs[:, 512:640],
-                    rhs=zc[:, 0:512].bitcast(FP8X4), rhs_scale=zs[:, 0:512],
-                    start=True, stop=True,
-                )
+                nc.tensor.matmul(out=acc_a[:], lhsT=zb[:, 0:P], rhs=zb[:], start=True, stop=True)
 
         state = {}
 
         def regroup_e(g):
             en = nat[g][0]
             er = rg.tile([P, 6, CS, D], BF16, name="er", tag="er")
-            nc.vector.tensor_copy(out=er[:], in_=en[:].rearrange("p c (r d) -> p r c d", d=D))
+            step = 2 if g == 0 else CS
+            for c in range(0, CS, step):
+                nc.vector.tensor_copy(
+                    out=er[:, :, c:c + step, :], in_=en[:, c:c + step, :].rearrange("p c (r d) -> p r c d", d=D)
+                )
             state[("re", g)] = er[:].rearrange("p r c d -> p (r c d)").bitcast(F32)
 
         def regroup_w(g):
@@ -107,17 +105,36 @@ def tile_vrtconv_kernel(tc, Ec, W1, W2, W3, b1, b2, b3, out):
             w1f, w2f, w3f = state.get(("rw", g), (None, None, None))
             grf = gr[:].bitcast(F32).rearrange("p (n x c u) -> p n x c u", n=6, x=2, u=2)
             stat = [(w1f, 0), (w2f, 0), (w2f, 1), (w3f, 0), (w3f, 1), (w3f, 2)]
-            for n in range(lo, hi):
-                tp = tpp.tile([P, 2, 2, P], F32, name="tp", tag="tp")
-                for x in range(2):
-                    for u in range(2):
-                        if n < 3:
-                            src, win = erf, (3 * x + n) * 2 + u
-                        else:
-                            src, a = stat[2 * (n - 3) + x]
-                            win = a * 2 + u
-                        nc.tensor.transpose(out=tp[:, x, u, :], in_=src[:, win * P:(win + 1) * P], identity=identf[:])
+
+            def one(tp, n, x, u):
+                if n < 3:
+                    src, win = erf, (3 * x + n) * 2 + u
+                else:
+                    src, a = stat[2 * (n - 3) + x]
+                    win = a * 2 + u
+                nc.tensor.transpose(out=tp[:, x, u, :], in_=src[:, win * P:(win + 1) * P], identity=identf[:])
+
+            def drain(tp, n):
                 nc.scalar.copy(out=grf[:, n], in_=tp[:].rearrange("p x u c -> p x c u"))
+
+            if g == 0 and lo == 0:
+                tps = []
+                for n in range(lo, hi):
+                    tp = tpp.tile([P, 2, 2, P], F32, name="tp", tag="tp")
+                    for x in range(2):
+                        one(tp, n, x, 0)
+                    tps.append(tp)
+                for n in range(lo, hi):
+                    for x in range(2):
+                        one(tps[n], n, x, 1)
+                    drain(tps[n], n)
+            else:
+                for n in range(lo, hi):
+                    tp = tpp.tile([P, 2, 2, P], F32, name="tp", tag="tp")
+                    for x in range(2):
+                        for u in range(2):
+                            one(tp, n, x, u)
+                    drain(tp, n)
 
         def quantise(g, half):
             gr = state[("g", g)]
@@ -156,22 +173,47 @@ def tile_vrtconv_kernel(tc, Ec, W1, W2, W3, b1, b2, b3, out):
                 mx(acc_d, 4, 256, 512, False, False)
                 mx(acc_d, 5, 512, 768, False, last)
 
+        def first_pos_v(name, src, h):
+            t = const.tile([P, 256], F32, name=name)
+            nc.vector.tensor_scalar(
+                out=t[:], in0=src, scalar1=bias[:, h:h + 1], scalar2=0.0, op0=ALU.add, op1=ALU.max
+            )
+            return t
+
+        def first_pos_s(name, src, h):
+            t = const.tile([P, 256], F32, name=name)
+            nc.scalar.activation(out=t[:], in_=src, func=ACT.Relu, bias=bias[:, h:h + 1], scale=1.0)
+            return t
+
+        def next_pos(name, src, h, prev):
+            t = const.tile([P, 256], F32, name=name)
+            nc.vector.scalar_tensor_tensor(out=t[:], in0=src, scalar=bias[:, h:h + 1], in1=prev[:], op0=ALU.add, op1=ALU.max)
+            return t
+
         ctx.enter_context(tc.manual_schedule())
-        idle_passes(10)
+        idle_matmuls(9)
         regroup_e(0)
         transposes(0, 0, 3)
-        idle_passes(2)
+        idle_matmuls(2)
         regroup_w(0)
         transposes(0, 3, 6)
-        idle_passes(2)
+        idle_matmuls(2)
         regroup_e(1)
         transposes(1, 0, 3)
+        idle_matmuls(2)
         for g in range(G):
             quantise(g, 0)
             passes(g, 0)
             if g + 1 < G:
                 regroup_w(g + 1)
                 transposes(g + 1, 3, 6)
+            else:
+                t1 = first_pos_v("t1", acc_a[:, 0:256], 0)
+                t1b = next_pos("t1b", acc_a[:, 256:512], 0, t1)
+                r1 = next_pos("r1", acc_b[:], 0, t1b)
+                tf = [tpp.tile([P, 3, P], F32, name="tf%d" % q, tag="tp") for q in range(2)]
+                for q in range(2):
+                    nc.tensor.transpose(out=tf[q][:, 0, :], in_=r1[:, q * P:(q + 1) * P], identity=identf[:])
             quantise(g, 1)
             passes(g, 1)
             if g + 2 < G:
@@ -182,32 +224,18 @@ def tile_vrtconv_kernel(tc, Ec, W1, W2, W3, b1, b2, b3, out):
                 nc.tensor.transpose(out=tpb[:], in_=bz[:], identity=identb[:])
                 nc.scalar.copy(out=bias[:, 0:3], in_=tpb[:, 0:3])
 
-        def first_pos(name, src, h):
-            t = const.tile([P, 256], F32, name=name)
-            nc.scalar.activation(out=t[:], in_=src, func=ACT.Relu, bias=bias[:, h:h + 1], scale=1.0)
-            return t
-
-        def next_pos(name, src, h, prev):
-            t = const.tile([P, 256], F32, name=name)
-            nc.vector.scalar_tensor_tensor(out=t[:], in0=src, scalar=bias[:, h:h + 1], in1=prev[:], op0=ALU.add, op1=ALU.max)
-            return t
-
-        t1 = first_pos("t1", acc_a[:, 0:256], 0)
-        t1b = next_pos("t1b", acc_a[:, 256:512], 0, t1)
-        r1 = next_pos("r1", acc_b[:], 0, t1b)
-        t2 = first_pos("t2", acc_c[:, 0:256], 1)
+        t2 = first_pos_s("t2", acc_c[:, 0:256], 1)
         r2 = next_pos("r2", acc_c[:, 256:512], 1, t2)
-        r3 = first_pos("r3", acc_d[:], 2)
-        res = [r1, r2, r3]
+        r3 = first_pos_s("r3", acc_d[:], 2)
 
         gout = const.tile([P, 32, 2, 12], F32, name="gout")
-        for q in range(2):
-            tf = tpp.tile([P, 3, P], F32, name="tf", tag="tp")
-            for h in range(3):
-                nc.tensor.transpose(out=tf[:, h, :], in_=res[h][:, q * P:(q + 1) * P], identity=identf[:])
-            nc.vector.tensor_copy(
+        for h, r in ((1, r2), (2, r3)):
+            for q in range(2):
+                nc.tensor.transpose(out=tf[q][:, h, :], in_=r[:, q * P:(q + 1) * P], identity=identf[:])
+        for q, copy in ((0, nc.vector.tensor_copy), (1, nc.scalar.copy)):
+            copy(
                 out=gout[:, :, q, :].rearrange("p o (j h) -> p o j h", h=3),
-                in_=tf[:].rearrange("p h (j o) -> p o j h", o=32),
+                in_=tf[q][:].rearrange("p h (j o) -> p o j h", o=32),
             )
         nc.sync.dma_start(
             out=out.rearrange("o (p q) z k -> p o (q z k)", q=2),

@@ -30,18 +30,15 @@ def tile_vrtconv_kernel(tc, Ec, W1, W2, W3, b1, b2, b3, out):
         accp = ctx.enter_context(tc.psum_pool(name="accp", bufs=1))
         tpp = ctx.enter_context(tc.psum_pool(name="tpp", bufs=4))
 
-        ec_v = Ec.rearrange("c (p q) l d -> p c (q l d)", q=2)
+        ec_v = Ec.rearrange("(g x e) (p q) l d -> g x p e (q l d)", x=2, e=2, q=4)
         w_v = [w.rearrange("j o c a d -> (j o) (c a d)") for w in (W1, W2, W3)]
 
 
         nat = []
         for g in range(G):
-            en = ld.tile([P, CS, 6 * D], BF16, name="en", tag="en")
-            if g == 0:
-                for u in range(2):
-                    nc.sync.dma_start(out=en[:, 2 * u:2 * u + 2, :], in_=ec_v[:, 2 * u:2 * u + 2, :])
-            else:
-                nc.sync.dma_start(out=en[:], in_=ec_v[:, g * CS:(g + 1) * CS, :])
+            en = ld.tile([P, 2, 12 * D], BF16, name="en", tag="en")
+            for x in range(2):
+                nc.sync.dma_start(out=en[x:P:2, :, :], in_=ec_v[g, x])
             wn = []
             for h in range(3):
                 wid = CS * (h + 1) * D
@@ -76,13 +73,9 @@ def tile_vrtconv_kernel(tc, Ec, W1, W2, W3, b1, b2, b3, out):
 
         def regroup_e(g):
             en = nat[g][0]
-            er = rg.tile([P, 6, CS, D], BF16, name="er", tag="er")
-            step = 2 if g == 0 else CS
-            for c in range(0, CS, step):
-                nc.vector.tensor_copy(
-                    out=er[:, :, c:c + step, :], in_=en[:, c:c + step, :].rearrange("p c (r d) -> p r c d", d=D)
-                )
-            state[("re", g)] = er[:].rearrange("p r c d -> p (r c d)").bitcast(F32)
+            er = rg.tile([P, 12, 2, D], BF16, name="er", tag="er")
+            nc.vector.tensor_copy(out=er[:], in_=en[:].rearrange("p e (r d) -> p r e d", d=D))
+            state[("re", g)] = er[:].rearrange("p r e d -> p (r e d)").bitcast(F32)
 
         def regroup_w(g):
             wn = nat[g][1]
@@ -103,38 +96,28 @@ def tile_vrtconv_kernel(tc, Ec, W1, W2, W3, b1, b2, b3, out):
             gr = state[("g", g)]
             erf = state[("re", g)]
             w1f, w2f, w3f = state.get(("rw", g), (None, None, None))
-            grf = gr[:].bitcast(F32).rearrange("p (n x c u) -> p n x c u", n=6, x=2, u=2)
+            grf = gr[:].bitcast(F32).rearrange("p (n w) -> p n w", n=6)
             stat = [(w1f, 0), (w2f, 0), (w2f, 1), (w3f, 0), (w3f, 1), (w3f, 2)]
 
-            def one(tp, n, x, u):
+            for n in range(lo, hi):
+                tp = tpp.tile([P, 4, P], F32, name="tp", tag="tp")
+                for i in range(4):
+                    if n < 3:
+                        src, win = erf, 3 * i + n
+                    else:
+                        src, a = stat[2 * (n - 3) + i // 2]
+                        win = 2 * a + i % 2
+                    nc.tensor.transpose(out=tp[:, i, :], in_=src[:, win * P:(win + 1) * P], identity=identf[:])
                 if n < 3:
-                    src, win = erf, (3 * x + n) * 2 + u
+                    nc.scalar.copy(
+                        out=grf[:, n].rearrange("k (p q x) -> k p q x", q=4, x=2),
+                        in_=tp[:].rearrange("k q (p x) -> k p q x", x=2),
+                    )
                 else:
-                    src, a = stat[2 * (n - 3) + x]
-                    win = a * 2 + u
-                nc.tensor.transpose(out=tp[:, x, u, :], in_=src[:, win * P:(win + 1) * P], identity=identf[:])
-
-            def drain(tp, n):
-                nc.scalar.copy(out=grf[:, n], in_=tp[:].rearrange("p x u c -> p x c u"))
-
-            if g == 0 and lo == 0:
-                tps = []
-                for n in range(lo, hi):
-                    tp = tpp.tile([P, 2, 2, P], F32, name="tp", tag="tp")
-                    for x in range(2):
-                        one(tp, n, x, 0)
-                    tps.append(tp)
-                for n in range(lo, hi):
-                    for x in range(2):
-                        one(tps[n], n, x, 1)
-                    drain(tps[n], n)
-            else:
-                for n in range(lo, hi):
-                    tp = tpp.tile([P, 2, 2, P], F32, name="tp", tag="tp")
-                    for x in range(2):
-                        for u in range(2):
-                            one(tp, n, x, u)
-                    drain(tp, n)
+                    nc.scalar.copy(
+                        out=grf[:, n].rearrange("k (a m u) -> k a m u", a=2, u=2),
+                        in_=tp[:].rearrange("k (a u) m -> k a m u", u=2),
+                    )
 
         def quantise(g, half):
             gr = state[("g", g)]
@@ -173,14 +156,7 @@ def tile_vrtconv_kernel(tc, Ec, W1, W2, W3, b1, b2, b3, out):
                 mx(acc_d, 4, 256, 512, False, False)
                 mx(acc_d, 5, 512, 768, False, last)
 
-        def first_pos_v(name, src, h):
-            t = const.tile([P, 256], F32, name=name)
-            nc.vector.tensor_scalar(
-                out=t[:], in0=src, scalar1=bias[:, h:h + 1], scalar2=0.0, op0=ALU.add, op1=ALU.max
-            )
-            return t
-
-        def first_pos_s(name, src, h):
+        def first_pos(name, src, h):
             t = const.tile([P, 256], F32, name=name)
             nc.scalar.activation(out=t[:], in_=src, func=ACT.Relu, bias=bias[:, h:h + 1], scale=1.0)
             return t
@@ -208,12 +184,7 @@ def tile_vrtconv_kernel(tc, Ec, W1, W2, W3, b1, b2, b3, out):
                 regroup_w(g + 1)
                 transposes(g + 1, 3, 6)
             else:
-                t1 = first_pos_v("t1", acc_a[:, 0:256], 0)
-                t1b = next_pos("t1b", acc_a[:, 256:512], 0, t1)
-                r1 = next_pos("r1", acc_b[:], 0, t1b)
-                tf = [tpp.tile([P, 3, P], F32, name="tf%d" % q, tag="tp") for q in range(2)]
-                for q in range(2):
-                    nc.tensor.transpose(out=tf[q][:, 0, :], in_=r1[:, q * P:(q + 1) * P], identity=identf[:])
+                t1 = first_pos("t1", acc_a[:, 0:256], 0)
             quantise(g, 1)
             passes(g, 1)
             if g + 2 < G:
@@ -224,14 +195,17 @@ def tile_vrtconv_kernel(tc, Ec, W1, W2, W3, b1, b2, b3, out):
                 nc.tensor.transpose(out=tpb[:], in_=bz[:], identity=identb[:])
                 nc.scalar.copy(out=bias[:, 0:3], in_=tpb[:, 0:3])
 
-        t2 = first_pos_s("t2", acc_c[:, 0:256], 1)
+        t1b = next_pos("t1b", acc_a[:, 256:512], 0, t1)
+        r1 = next_pos("r1", acc_b[:], 0, t1b)
+        t2 = first_pos("t2", acc_c[:, 0:256], 1)
         r2 = next_pos("r2", acc_c[:, 256:512], 1, t2)
-        r3 = first_pos_s("r3", acc_d[:], 2)
+        r3 = first_pos("r3", acc_d[:], 2)
+        tf = [tpp.tile([P, 3, P], F32, name="tf%d" % q, tag="tp") for q in range(2)]
 
         gout = const.tile([P, 32, 2, 12], F32, name="gout")
-        for h, r in ((1, r2), (2, r3)):
+        for h, r in enumerate((r1, r2, r3)):
             for q in range(2):
-                nc.tensor.transpose(out=tf[q][:, h, :], in_=r[:, q * P:(q + 1) * P], identity=identf[:])
+                nc.tensor.transpose(out=tf[q][:, h, :], in_=r[:, q:256:2], identity=identf[:])
         for q, copy in ((0, nc.vector.tensor_copy), (1, nc.scalar.copy)):
             copy(
                 out=gout[:, :, q, :].rearrange("p o (j h) -> p o j h", h=3),

@@ -82,7 +82,9 @@ def tile_vrtconv_kernel(tc, Ec, W1, W2, W3, b1, b2, b3, out):
             w2r = rg.tile([P, 2, CS, D], BF16, name="w2r", tag="w2r")
             nc.vector.tensor_copy(out=w2r[:], in_=wn[1][:].rearrange("p (c a d) -> p a c d", a=2, d=D))
             w3r = rg.tile([P, 3, CS, D], BF16, name="w3r", tag="w3r")
-            nc.vector.tensor_copy(out=w3r[:], in_=wn[2][:].rearrange("p (c a d) -> p a c d", a=3, d=D))
+            nc.vector.tensor_copy(
+                out=w3r[:].rearrange("p a c d -> p c a d"), in_=wn[2][:].rearrange("p (c a d) -> p c a d", a=3, d=D)
+            )
             state[("rw", g)] = (
                 wn[0][:].bitcast(F32),
                 w2r[:].rearrange("p a c d -> p (a c d)").bitcast(F32),

@@ -202,18 +202,24 @@ def tile_vrtconv_kernel(tc, Ec, W1, W2, W3, b1, b2, b3, out):
         t2 = first_pos("t2", acc_c[:, 0:256], 1)
         r2 = next_pos("r2", acc_c[:, 256:512], 1, t2)
         r3 = first_pos("r3", acc_d[:], 2)
-        tf = [tpp.tile([P, 3, P], F32, name="tf%d" % q, tag="tp") for q in range(2)]
-
-        gout = const.tile([P, 32, 2, 12], F32, name="gout")
+        tfa = tpp.tile([P, 2, 2, P], F32, name="tfa", tag="tp")
+        tfb = tpp.tile([P, 2, P], F32, name="tfb", tag="tp")
+        xt = const.tile([P, 3, 2, 4, 32], F32, name="xt", align_bytes=64)
+        gout = const.tile([P, 64, 12], F32, name="gout")
         for h, r in enumerate((r1, r2, r3)):
-            for q in range(2):
-                nc.tensor.transpose(out=tf[q][:, h, :], in_=r[:, q:256:2], identity=identf[:])
-        for q, copy in ((0, nc.vector.tensor_copy), (1, nc.scalar.copy)):
-            copy(
-                out=gout[:, :, q, :].rearrange("p o (j h) -> p o j h", h=3),
-                in_=tf[q][:].rearrange("p h (j o) -> p o j h", o=32),
-            )
-        nc.sync.dma_start(
-            out=out.rearrange("o (p q) z k -> p o (q z k)", q=2),
-            in_=gout[:].rearrange("p o q k -> p o (q k)"),
-        )
+            for t in range(2):
+                tf = tfa[:, h, t, :] if h < 2 else tfb[:, t, :]
+                nc.tensor.transpose(out=tf, in_=r[:, t:256:2], identity=identf[:])
+            if h == 1:
+                nc.vector.transpose(
+                    out=xt[:, 0:2].rearrange("p h t j i -> p (h t j i)"), in_=tfa[:].rearrange("p h t m -> p (h t m)")
+                )
+        for t in range(2):
+            nc.vector.transpose(out=xt[:, 2, t].rearrange("p j i -> p (j i)"), in_=tfb[:, t, :])
+        gv = gout[:].rearrange("p (i t) (j h) -> p i t j h", t=2, h=3)
+        xv = xt[:].rearrange("p h t j i -> p i t j h")
+        ov = out.rearrange("o (b s) z k -> b o (s z k)", b=4)
+        for copy, lo, hi in ((nc.vector.tensor_copy, 0, 16), (nc.scalar.copy, 16, 32)):
+            copy(out=gv[:, lo:hi].rearrange("p i t j h -> p i (t j) h"), in_=xv[:, lo:hi].rearrange("p i t j h -> p i (t j) h"))
+        for b, dma in enumerate((nc.sync, nc.scalar, nc.sync, nc.scalar)):
+            dma.dma_start(out=ov[b], in_=gout[32 * b:32 * b + 32].rearrange("p s k -> p (s k)"))

from contextlib import ExitStack

import concourse.mybir as mybir
from concourse.masks import make_identity

BF16 = mybir.dt.bfloat16
F32 = mybir.dt.float32
U32 = mybir.dt.uint32
U8 = mybir.dt.uint8
I32 = mybir.dt.int32
FP8X4 = mybir.dt.float8_e4m3fn_x4
ALU = mybir.AluOpType
ACT = mybir.ActivationFunctionType

P = 128
C, S, L, D = 32, 256, 3, 128
CS = 4
G = C // CS
FLOPS = 2 * 128 * (768 * 4096 + 512 * 8192 + 256 * 12288)


def tile_vrtconv_kernel(tc, Ec, W1, W2, W3, b1, b2, b3, out):
    nc = tc.nc
    with ExitStack() as ctx:
        const = ctx.enter_context(tc.tile_pool(name="const", bufs=1))
        ld = ctx.enter_context(tc.tile_pool(name="ld", bufs=G))
        rg = ctx.enter_context(tc.tile_pool(name="rg", bufs=2))
        grp = ctx.enter_context(tc.tile_pool(name="grp", bufs=2))
        keep = ctx.enter_context(tc.tile_pool(name="keep", bufs=3))
        accp = ctx.enter_context(tc.psum_pool(name="accp", bufs=1))
        tpp = ctx.enter_context(tc.psum_pool(name="tpp", bufs=4))

        ec_v = Ec.rearrange("(g x e) (p q) l d -> g x p e (q l d)", x=2, e=2, q=4)
        w_v = [w.rearrange("j o c a d -> (j o) (c a d)") for w in (W1, W2, W3)]


        nat = []
        for g in range(G):
            en = ld.tile([P, 2, 12 * D], BF16, name="en", tag="en")
            for x in range(2):
                nc.sync.dma_start(out=en[x:P:2, :, :], in_=ec_v[g, x])
            wn = []
            for h in range(3):
                wid = CS * (h + 1) * D
                t = ld.tile([P, wid], BF16, name="wn%d" % h, tag="wn%d" % h)
                nc.sync.dma_start(out=t[:], in_=w_v[h][:, g * wid:(g + 1) * wid])
                wn.append(t)
            nat.append((en, wn))

        identf = const.tile([P, P], F32, name="identf")
        make_identity(nc, identf[:])
        identb = const.tile([P, P], BF16, name="identb")
        make_identity(nc, identb[:])
        bias = const.tile([P, 4], F32, name="bias")
        bz = const.tile([P, P], BF16, name="bz")
        nc.gpsimd.memset(bz[:], 0.0)
        for h, b in enumerate((b1, b2, b3)):
            nc.gpsimd.dma_start(out=bz[h:h + 1, :], in_=b.rearrange("(x j) o -> x (j o)", x=1))

        acc_a = accp.tile([P, 512], F32, name="acc_a")
        acc_b = accp.tile([P, 256], F32, name="acc_b")
        acc_c = accp.tile([P, 512], F32, name="acc_c")
        acc_d = accp.tile([P, 256], F32, name="acc_d")

        zb = const.tile([P, 512], BF16, name="zb")
        nc.vector.memset(zb[:].bitcast(I32), 0)

        def idle_matmuls(n):
            for i in range(n):
                nc.tensor.matmul(out=acc_a[:], lhsT=zb[:, 0:P], rhs=zb[:], start=True, stop=True)

        state = {}

        def regroup_e(g):
            en = nat[g][0]
            er = rg.tile([P, 12, 2, D], BF16, name="er", tag="er")
            nc.vector.tensor_copy(out=er[:], in_=en[:].rearrange("p e (r d) -> p r e d", d=D))
            state[("re", g)] = er[:].rearrange("p r e d -> p (r e d)").bitcast(F32)

        def regroup_w(g):
            wn = nat[g][1]
            w2r = rg.tile([P, 2, CS, D], BF16, name="w2r", tag="w2r")
            nc.vector.tensor_copy(out=w2r[:], in_=wn[1][:].rearrange("p (c a d) -> p a c d", a=2, d=D))
            w3r = rg.tile([P, 3, CS, D], BF16, name="w3r", tag="w3r")
            nc.vector.tensor_copy(
                out=w3r[:].rearrange("p a c d -> p c a d"), in_=wn[2][:].rearrange("p (c a d) -> p c a d", a=3, d=D)
            )
            state[("rw", g)] = (
                wn[0][:].bitcast(F32),
                w2r[:].rearrange("p a c d -> p (a c d)").bitcast(F32),
                w3r[:].rearrange("p a c d -> p (a c d)").bitcast(F32),
            )

        def transposes(g, lo, hi):
            if lo == 0:
                gr = grp.tile([P, 6 * 1024], BF16, name="gr", tag="gr", align_bytes=64)
                state[("g", g)] = gr
            gr = state[("g", g)]
            erf = state[("re", g)]
            w1f, w2f, w3f = state.get(("rw", g), (None, None, None))
            grf = gr[:].bitcast(F32).rearrange("p (n w) -> p n w", n=6)
            stat = [(w1f, 0), (w2f, 0), (w2f, 1), (w3f, 0), (w3f, 1), (w3f, 2)]

            for n in range(lo, hi):
                tp = tpp.tile([P, 4, P], F32, name="tp", tag="tp")
                for i in range(4):
                    if n < 3:
                        src, win = erf, 3 * i + n
                    else:
                        src, a = stat[2 * (n - 3) + i // 2]
                        win = 2 * a + i % 2
                    nc.tensor.transpose(out=tp[:, i, :], in_=src[:, win * P:(win + 1) * P], identity=identf[:])
                if n < 3:
                    nc.scalar.copy(
                        out=grf[:, n].rearrange("k (p q x) -> k p q x", q=4, x=2),
                        in_=tp[:].rearrange("k q (p x) -> k p q x", x=2),
                    )
                else:
                    nc.scalar.copy(
                        out=grf[:, n].rearrange("k (a m u) -> k a m u", a=2, u=2),
                        in_=tp[:].rearrange("k (a u) m -> k a m u", u=2),
                    )

        def quantise(g, half):
            gr = state[("g", g)]
            if half == 0:
                cd = keep.tile([P, 1536], U32, name="cd", tag="cd", align_bytes=64)
                sc = keep.tile([P, 1536], U8, name="sc", tag="sc", align_bytes=64)
                state[("q", g)] = (cd, sc)
            cd, sc = state[("q", g)]
            lo, hi = (0, 1024) if half == 0 else (1024, 1536)
            step = (hi - lo) // 2 if g == G - 1 else hi - lo
            for w in range(lo, hi, step):
                nc.vector.quantize_mx(
                    out=cd[:, w:w + step].bitcast(FP8X4), scales=sc[:, w:w + step], in_=gr[:, 4 * w:4 * (w + step)]
                )

        def passes(g, half):
            cd, sc = state[("q", g)]
            first, last = g == 0, g == G - 1

            def mx(acc, i, lo, hi, start, stop):
                w0 = 768 + P * i
                nc.tensor.matmul_mx(
                    out=acc[:],
                    lhsT=cd[:, w0:w0 + P].bitcast(FP8X4), lhsT_scale=sc[:, w0:w0 + P],
                    rhs=cd[:, lo:hi].bitcast(FP8X4), rhs_scale=sc[:, lo:hi],
                    start=start, stop=stop,
                )

            if half == 0:
                mx(acc_a, 0, 0, 512, first, last)
                mx(acc_b, 0, 512, 768, first, last)
                mx(acc_c, 1, 0, 512, first, False)
            else:
                mx(acc_c, 2, 256, 768, False, last)
                mx(acc_d, 3, 0, 256, first, False)
                mx(acc_d, 4, 256, 512, False, False)
                mx(acc_d, 5, 512, 768, False, last)

        def first_pos(name, src, h):
            t = const.tile([P, 256], F32, name=name)
            nc.scalar.activation(out=t[:], in_=src, func=ACT.Relu, bias=bias[:, h:h + 1], scale=1.0)
            return t

        def next_pos(name, src, h, prev):
            t = const.tile([P, 256], F32, name=name)
            nc.vector.scalar_tensor_tensor(out=t[:], in0=src, scalar=bias[:, h:h + 1], in1=prev[:], op0=ALU.add, op1=ALU.max)
            return t

        ctx.enter_context(tc.manual_schedule())
        idle_matmuls(9)
        regroup_e(0)
        transposes(0, 0, 3)
        idle_matmuls(2)
        regroup_w(0)
        transposes(0, 3, 6)
        idle_matmuls(2)
        regroup_e(1)
        transposes(1, 0, 3)
        idle_matmuls(2)
        for g in range(G):
            quantise(g, 0)
            passes(g, 0)
            if g + 1 < G:
                regroup_w(g + 1)
                transposes(g + 1, 3, 6)
            else:
                t1 = first_pos("t1", acc_a[:, 0:256], 0)
            quantise(g, 1)
            passes(g, 1)
            if g + 2 < G:
                regroup_e(g + 2)
                transposes(g + 2, 0, 3)
            if g == 3:
                tpb = tpp.tile([P, P], BF16, name="tpb", tag="tp")
                nc.tensor.transpose(out=tpb[:], in_=bz[:], identity=identb[:])
                nc.scalar.copy(out=bias[:, 0:3], in_=tpb[:, 0:3])

        t1b = next_pos("t1b", acc_a[:, 256:512], 0, t1)
        r1 = next_pos("r1", acc_b[:], 0, t1b)
        t2 = first_pos("t2", acc_c[:, 0:256], 1)
        r2 = next_pos("r2", acc_c[:, 256:512], 1, t2)
        r3 = first_pos("r3", acc_d[:], 2)
        tfa = tpp.tile([P, 2, 2, P], F32, name="tfa", tag="tp")
        tfb = tpp.tile([P, 2, P], F32, name="tfb", tag="tp")
        xt = const.tile([P, 3, 2, 4, 32], F32, name="xt", align_bytes=64)
        gout = const.tile([P, 64, 12], F32, name="gout")
        for h, r in enumerate((r1, r2, r3)):
            for t in range(2):
                tf = tfa[:, h, t, :] if h < 2 else tfb[:, t, :]
                nc.tensor.transpose(out=tf, in_=r[:, t:256:2], identity=identf[:])
            if h == 1:
                nc.vector.transpose(
                    out=xt[:, 0:2].rearrange("p h t j i -> p (h t j i)"), in_=tfa[:].rearrange("p h t m -> p (h t m)")
                )
        for t in range(2):
            nc.vector.transpose(out=xt[:, 2, t].rearrange("p j i -> p (j i)"), in_=tfb[:, t, :])
        gv = gout[:].rearrange("p (i t) (j h) -> p i t j h", t=2, h=3)
        xv = xt[:].rearrange("p h t j i -> p i t j h")
        ov = out.rearrange("o (b s) z k -> b o (s z k)", b=4)
        for copy, lo, hi in ((nc.vector.tensor_copy, 0, 16), (nc.scalar.copy, 16, 32)):
            copy(out=gv[:, lo:hi].rearrange("p i t j h -> p i (t j) h"), in_=xv[:, lo:hi].rearrange("p i t j h -> p i (t j) h"))
        for b, dma in enumerate((nc.sync, nc.scalar, nc.sync, nc.scalar)):
            dma.dma_start(out=ov[b], in_=gout[32 * b:32 * b + 32].rearrange("p s k -> p (s k)"))
